import numpy as np
import ml_dtypes


def mxq(x, axis, fmt="e4m3"):
    dtype, down = {"e4m3": (ml_dtypes.float8_e4m3fn, 7), "e5m2": (ml_dtypes.float8_e5m2, 14)}[fmt]
    v = np.moveaxis(np.asarray(x, np.float32).astype(ml_dtypes.bfloat16).astype(np.float64), axis, -1)
    blocks = v.reshape(v.shape[:-1] + (-1, 32))
    amax = np.abs(blocks).max(-1, keepdims=True)
    byte = np.maximum(np.where(amax > 0, np.frexp(amax)[1] - 1 + 127, 0) - down, 1)
    scale = np.exp2(byte - 127.0)
    codes = (blocks / scale).astype(np.float32).astype(dtype).astype(np.float64)
    return np.moveaxis((codes * scale).reshape(v.shape), -1, axis)


WIDE = False


def mx_kscale(k):
    if not WIDE:
        return np.ones(k)
    levels = np.array([10, -10, 5, -5, 0])
    a = np.random.permutation(np.resize(levels, k // 512 * 4)).reshape(k // 512, 4)
    idx = np.arange(k)
    return np.exp2(a[idx // 512, idx % 128 // 32])


BF16 = ml_dtypes.bfloat16


def bf(x):
    return np.asarray(x, np.float32).astype(BF16)


def f64(x):
    return np.asarray(x).astype(np.float64)


M, DIN, D = 4096, 128, 512


def setup_inputs():
    s = mx_kscale(D)
    s = s / s.max()
    r = np.random.standard_normal
    return {"S": bf(r((M, D)) * s),
            "X": bf(r((M, DIN))),
            "Uz": bf(r((DIN, D)) * 0.5 / np.sqrt(DIN)),
            "Ug": bf(r((DIN, D)) * 0.5 / np.sqrt(DIN)),
            "Ur": bf(r((DIN, D)) * 0.5 / np.sqrt(DIN)),
            "Uh": bf(r((DIN, D)) * 0.5 / np.sqrt(DIN)),
            "Wz": bf(r((D, D)) * 0.7 / np.sqrt(D) / s[:, None]),
            "Wg": bf(r((D, D)) * 0.7 / np.sqrt(D) / s[:, None]),
            "Wr": bf(r((D, D)) * 0.7 / np.sqrt(D) / s[:, None]),
            "Wh": bf(r((D, D)) * 1.0 / np.sqrt(D) / s[:, None]),
            "bz": bf(r((1, D)) * 0.3),
            "bg": bf(r((1, D)) * 0.3),
            "br": bf(r((1, D)) * 0.3),
            "bh": bf(r((1, D)) * 0.3)}


def reference(S, X, Uz, Ug, Ur, Uh, Wz, Wg, Wr, Wh, bz, bg, br, bh):
    Sf = f64(S)
    Sq = mxq(Sf, 1, "e4m3")
    Z = np.tanh(f64(X) @ f64(Uz) + (Sq @ mxq(f64(Wz), 0, "e4m3")) + f64(bz))
    G = np.tanh(f64(X) @ f64(Ug) + (Sq @ mxq(f64(Wg), 0, "e4m3")) + f64(bg))
    R = np.tanh(f64(X) @ f64(Ur) + (Sq @ mxq(f64(Wr), 0, "e4m3")) + f64(br))
    SR = Sf * R
    H = np.tanh(f64(X) @ f64(Uh) + (mxq(SR, 1, "e4m3") @ mxq(f64(Wh), 0, "e4m3")) + f64(bh))
    return (1.0 - G) * H + Z * Sf

@@ -1,0 +1,333 @@
+from contextlib import ExitStack
+
+import concourse.mybir as mybir
+from concourse.masks import make_identity
+
+F32 = mybir.dt.float32
+BF16 = mybir.dt.bfloat16
+U32 = mybir.dt.uint32
+U8 = mybir.dt.uint8
+FP8X4 = mybir.dt.float8_e4m3fn_x4
+ALU = mybir.AluOpType
+ACT = mybir.ActivationFunctionType
+
+M, DIN, D = 4096, 128, 512
+P = 128
+PACK = 4
+TOKENS = 512
+BLOCKS = 4
+ROUNDS = M // TOKENS
+BY_FEATURE = ("r", "g", "h")
+TANH_LAG = 2
+
+FLOPS = 2 * M * D * 4 * (D + DIN)
+
+
+def tile_lstmlayer_pa_t_kernel(
+    tc, S, X, Uz, Ug, Ur, Uh, Wz, Wg, Wr, Wh, bz, bg, br, bh, out
+):
+    nc = tc.nc
+    w_dram = {"r": Wr, "z": Wz, "g": Wg, "h": Wh}
+    u_dram = {"r": Ur, "z": Uz, "g": Ug, "h": Uh}
+    b_dram = {"r": br, "g": bg, "h": bh}
+
+    s_rounds = S.rearrange("(s p j) d -> s p j d", p=P, j=BLOCKS)
+    x_rounds = X.rearrange("(s p j) d -> s p j d", p=P, j=BLOCKS)
+    out_rounds = out.rearrange("(s p j) d -> s p j d", p=P, j=BLOCKS)
+
+    with ExitStack() as ctx:
+        ctx.enter_context(tc.manual_schedule())
+        const = ctx.enter_context(tc.tile_pool(name="const", bufs=1))
+        stage = ctx.enter_context(tc.tile_pool(name="stage", bufs=4))
+        loads = ctx.enter_context(tc.tile_pool(name="loads", bufs=3))
+        work = ctx.enter_context(tc.tile_pool(name="work", bufs=2))
+        psum_plain = ctx.enter_context(tc.psum_pool(name="psum_plain", bufs=2))
+        psum_mx = ctx.enter_context(tc.psum_pool(name="psum_mx", bufs=2))
+        psum_t = ctx.enter_context(tc.psum_pool(name="psum_t", bufs=4))
+
+        w_raw = {}
+        u_raw = {}
+        w_codes = {}
+        w_scales = {}
+        u_ready = {}
+        s_nat = {}
+        x_nat = {}
+        s_grouped = {}
+        s_codes = {}
+        s_scales = {}
+        x_t = {}
+        sr_grouped = {}
+        sr_codes = {}
+        sr_scales = {}
+        gate_tile = {}
+
+        def load_gate(gate):
+            w_raw[gate] = stage.tile([P, PACK, D], BF16, name="w_raw")
+            nc.sync.dma_start(
+                out=w_raw[gate][:].rearrange("x (u e) c -> x u e c", u=2),
+                in_=w_dram[gate].rearrange("(u x e) c -> x u e c", u=2, e=2),
+            )
+            u_raw[gate] = const.tile([P, D], BF16, name="u_raw_%s" % gate)
+            nc.sync.dma_start(out=u_raw[gate][:], in_=u_dram[gate])
+
+        def load_round(s):
+            s_nat[s] = loads.tile([P, BLOCKS, D], BF16, name="s_nat")
+            nc.sync.dma_start(out=s_nat[s][:], in_=s_rounds[s])
+            x_nat[s] = loads.tile([P, BLOCKS, DIN], BF16, name="x_nat")
+            nc.sync.dma_start(out=x_nat[s][:], in_=x_rounds[s])
+
+        def prepare_gate(gate):
+            w_grouped = stage.tile([P, D, PACK], BF16, align_bytes=64, bufs=2)
+            if gate == "r":
+                for u in range(2):
+                    half = slice(2 * P * u, 2 * P * (u + 1))
+                    nc.vector.tensor_copy(
+                        out=w_grouped[:, half, :].rearrange("x (e c) t -> x e c t", e=2),
+                        in_=w_raw[gate][:, :, half].rearrange("x t (c e) -> x e c t", e=2),
+                    )
+                u_ready[gate] = const.tile([P, D], BF16, name="u_sorted")
+                nc.vector.tensor_copy(
+                    out=u_ready[gate][:].rearrange("k (u e c) -> k u e c", u=2, e=2),
+                    in_=u_raw[gate][:].rearrange("k (u c e) -> k u e c", u=2, e=2),
+                )
+            else:
+                nc.vector.tensor_copy(
+                    out=w_grouped[:], in_=w_raw[gate][:].rearrange("x t c -> x c t")
+                )
+                u_ready[gate] = u_raw[gate]
+            w_codes[gate] = const.tile([P, D], U32, name="w_codes_%s" % gate, align_bytes=64)
+            w_scales[gate] = const.tile([P, D], U8, name="w_scales_%s" % gate, align_bytes=64)
+            nc.vector.quantize_mx(
+                out=w_codes[gate][:].bitcast(FP8X4),
+                scales=w_scales[gate][:],
+                in_=w_grouped[:].rearrange("x c t -> x (c t)"),
+            )
+
+        def transpose_in(s):
+            s_grouped[s] = work.tile([P, TOKENS, PACK], BF16, name="s_grouped", align_bytes=64)
+            s_words = (
+                s_grouped[s][:]
+                .rearrange("x m t -> x (m t)")
+                .bitcast(F32)
+                .rearrange("x (m u) -> x m u", u=2)
+            )
+            s_banks = []
+            for pair in range(BLOCKS // 2):
+                s_bank = psum_t.tile([P, 2, 2 * P], F32, tag="t")
+                for u in range(2):
+                    for i in range(2):
+                        nc.tensor.transpose(
+                            out=s_bank[:, u, P * i : P * (i + 1)],
+                            in_=s_nat[s][:, 2 * pair + i, :].bitcast(F32)[:, P * u : P * (u + 1)],
+                            identity=ident_f32[:],
+                        )
+                s_banks.append(s_bank)
+            x_bank = psum_t.tile([P, TOKENS], BF16, tag="t")
+            for j in range(BLOCKS):
+                nc.tensor.transpose(
+                    out=x_bank[:, P * j : P * (j + 1)],
+                    in_=x_nat[s][:, j, :],
+                    identity=ident_bf16[:],
+                )
+            for pair in range(BLOCKS // 2):
+                nc.scalar.copy(
+                    out=s_words[:, 2 * P * pair : 2 * P * (pair + 1), :],
+                    in_=s_banks[pair][:].rearrange("x u m -> x m u"),
+                )
+            x_t[s] = work.tile([P, TOKENS], BF16, name="x_t")
+            nc.scalar.copy(out=x_t[s][:], in_=x_bank[:])
+
+        def quantise_s(s):
+            s_codes[s] = work.tile([P, TOKENS], U32, name="s_codes", align_bytes=64)
+            s_scales[s] = work.tile([P, TOKENS], U8, name="s_scales", align_bytes=64)
+            nc.vector.quantize_mx(
+                out=s_codes[s][:].bitcast(FP8X4),
+                scales=s_scales[s][:],
+                in_=s_grouped[s][:].rearrange("x m t -> x (m t)"),
+            )
+
+        def quantise_sr(s):
+            sr_codes[s] = work.tile([P, TOKENS], U32, name="sr_codes", align_bytes=64)
+            sr_scales[s] = work.tile([P, TOKENS], U8, name="sr_scales", align_bytes=64)
+            nc.vector.quantize_mx(
+                out=sr_codes[s][:].bitcast(FP8X4),
+                scales=sr_scales[s][:],
+                in_=sr_grouped[s][:].rearrange("x m t -> x (m t)"),
+            )
+
+        def sums(gate, s, b):
+            if b == 0:
+                gate_tile[gate, s] = work.tile(
+                    [P, BLOCKS, D if gate == "z" else TOKENS],
+                    F32,
+                    name=gate,
+                    bufs=3 if gate == "z" else 2,
+                )
+            block = slice(P * b, P * (b + 1))
+            if gate == "h":
+                act_codes, act_scales = sr_codes[s], sr_scales[s]
+            else:
+                act_codes, act_scales = s_codes[s], s_scales[s]
+            plain = psum_plain.tile([P, TOKENS], F32)
+            mx = psum_mx.tile([P, TOKENS], F32)
+            plain_sb = work.tile([P, TOKENS], F32, bufs=4)
+            if gate == "z":
+                nc.tensor.matmul(
+                    out=plain[:], lhsT=x_t[s][:, block], rhs=u_ready[gate][:], start=True, stop=True
+                )
+                nc.tensor.matmul_mx(
+                    out=mx[:],
+                    lhsT=act_codes[:, block].bitcast(FP8X4),
+                    lhsT_scale=act_scales[:, block],
+                    rhs=w_codes[gate][:].bitcast(FP8X4),
+                    rhs_scale=w_scales[gate][:],
+                    start=True,
+                    stop=True,
+                )
+                nc.vector.tensor_add(out=plain_sb[:], in0=plain[:], in1=bz_rows[:])
+            else:
+                nc.tensor.matmul(
+                    out=plain[:], lhsT=u_ready[gate][:, block], rhs=x_t[s][:], start=True, stop=True
+                )
+                nc.tensor.matmul_mx(
+                    out=mx[:],
+                    lhsT=w_codes[gate][:, block].bitcast(FP8X4),
+                    lhsT_scale=w_scales[gate][:, block],
+                    rhs=act_codes[:].bitcast(FP8X4),
+                    rhs_scale=act_scales[:],
+                    start=True,
+                    stop=True,
+                )
+                nc.scalar.copy(out=plain_sb[:], in_=plain[:])
+            nc.vector.tensor_add(out=gate_tile[gate, s][:, b, :], in0=mx[:], in1=plain_sb[:])
+
+        def tanh(gate, s, b):
+            values = gate_tile[gate, s][:, b, :]
+            if gate == "z":
+                nc.scalar.activation(out=values, in_=values, func=ACT.Tanh)
+                nc.gpsimd.tensor_tensor(out=values, in0=values, in1=s_nat[s][:, b, :], op=ALU.mult)
+            else:
+                index = BY_FEATURE.index(gate)
+                nc.scalar.activation(
+                    out=values, in_=values, func=ACT.Tanh, bias=b_col[gate][:, b, index : index + 1]
+                )
+            if gate == "r" and b == BLOCKS - 1:
+                sr_grouped[s] = work.tile(
+                    [P, TOKENS, PACK], BF16, name="sr_grouped", align_bytes=64
+                )
+                for i in range(2):
+                    part = slice(TOKENS // 2 * i, TOKENS // 2 * (i + 1))
+                    nc.gpsimd.tensor_tensor(
+                        out=sr_grouped[s][:, part, :],
+                        in0=s_grouped[s][:, part, :],
+                        in1=gate_tile[gate, s][:, :, part].rearrange("x t m -> x m t"),
+                        op=ALU.mult,
+                    )
+
+        started = []
+
+        def step(gate, s, b):
+            sums(gate, s, b)
+            started.append((gate, s, b))
+            if len(started) > TANH_LAG:
+                tanh(*started[len(started) - 1 - TANH_LAG])
+
+        def blend(s, t):
+            nc.vector.scalar_tensor_tensor(
+                out=gate_tile["g", s][:, t, :],
+                in0=gate_tile["g", s][:, t, :],
+                scalar=1.0,
+                in1=gate_tile["h", s][:, t, :],
+                op0=ALU.subtract,
+                op1=ALU.mult,
+            )
+
+        def finish(s, t):
+            back = psum_t.tile([P, BLOCKS, P], F32, tag="t")
+            for j in range(BLOCKS):
+                nc.tensor.transpose(
+                    out=back[:, j, :],
+                    in_=gate_tile["g", s][:, t, P * j : P * (j + 1)],
+                    identity=ident_f32[:],
+                )
+            columns = gate_tile["z", s][:, :, P * t : P * (t + 1)]
+            nc.vector.tensor_sub(out=columns, in0=columns, in1=back[:])
+
+        def store(s):
+            nc.sync.dma_start(out=out_rounds[s], in_=gate_tile["z", s][:])
+
+        load_gate("r")
+        load_round(0)
+        bias_rows = const.tile([P, D], BF16)
+        nc.vector.memset(bias_rows[:], 0.0)
+        for index, gate in enumerate(BY_FEATURE):
+            nc.sync.dma_start(out=bias_rows[index : index + 1, :], in_=b_dram[gate])
+        bz_rows = const.tile([P, D], BF16)
+        nc.sync.dma_start(out=bz_rows[:], in_=bz.rearrange("o d -> (o d)").partition_broadcast(P))
+        for gate in ("z", "g", "h"):
+            load_gate(gate)
+        load_round(1)
+
+        ident_f32 = const.tile([P, P], F32)
+        make_identity(nc, ident_f32[:])
+        ident_bf16 = const.tile([P, P], BF16)
+        make_identity(nc, ident_bf16[:])
+
+        prepare_gate("r")
+
+        bias_sorted = const.tile([P, D], BF16)
+        nc.vector.tensor_copy(
+            out=bias_sorted[:].rearrange("k (u e c) -> k u e c", u=2, e=2),
+            in_=bias_rows[:].rearrange("k (u c e) -> k u e c", u=2, e=2),
+        )
+
+        def bias_columns(rows, name):
+            bias_bank = psum_t.tile([P, BLOCKS, P], BF16, tag="t")
+            for t in range(BLOCKS):
+                nc.tensor.transpose(
+                    out=bias_bank[:, t, :], in_=rows[:, P * t : P * (t + 1)], identity=ident_bf16[:]
+                )
+            kept = const.tile([P, BLOCKS, len(BY_FEATURE)], F32, name=name)
+            nc.vector.tensor_copy(out=kept[:], in_=bias_bank[:, :, 0 : len(BY_FEATURE)])
+            return kept
+
+        b_sorted = bias_columns(bias_sorted, "b_sorted")
+        b_plain = bias_columns(bias_rows, "b_plain")
+        b_col = {"r": b_sorted, "g": b_plain, "h": b_plain}
+
+        transpose_in(0)
+        quantise_s(0)
+        for t in range(BLOCKS):
+            step("r", 0, t)
+            if t < 3:
+                prepare_gate(("z", "g", "h")[t])
+
+        for s in range(ROUNDS):
+            if s + 2 < ROUNDS:
+                load_round(s + 2)
+            if s + 1 < ROUNDS:
+                transpose_in(s + 1)
+            for b in range(BLOCKS):
+                step("z", s, b)
+                step("g", s, b)
+                if b == 0 and s + 1 < ROUNDS:
+                    quantise_s(s + 1)
+            quantise_sr(s)
+            for t in range(BLOCKS):
+                if s + 1 < ROUNDS:
+                    step("r", s + 1, t)
+                if s > 0:
+                    blend(s - 1, t)
+            for t in range(BLOCKS):
+                step("h", s, t)
+                if s > 0:
+                    finish(s - 1, t)
+            if s > 0:
+                store(s - 1)
+
+        for late in started[len(started) - TANH_LAG :]:
+            tanh(*late)
+        for t in range(BLOCKS):
+            blend(ROUNDS - 1, t)
+            finish(ROUNDS - 1, t)
+        store(ROUNDS - 1)

@@ -18,6 +18,7 @@ TOKENS = 512
 BLOCKS = 4
 ROUNDS = M // TOKENS
 BY_FEATURE = ("r", "g", "h")
+MX_LAG = 1
 TANH_LAG = 2
 
 FLOPS = 2 * M * D * 4 * (D + DIN)
@@ -60,6 +61,7 @@ def tile_lstmlayer_pa_t_kernel(
         sr_codes = {}
         sr_scales = {}
         gate_tile = {}
+        plain_sb = {}
 
         def load_gate(gate):
             w_raw[gate] = stage.tile([P, PACK, D], BF16, name="w_raw")
@@ -155,7 +157,7 @@ def tile_lstmlayer_pa_t_kernel(
                 in_=sr_grouped[s][:].rearrange("x m t -> x (m t)"),
             )
 
-        def sums(gate, s, b):
+        def plain_part(gate, s, b):
             if b == 0:
                 gate_tile[gate, s] = work.tile(
                     [P, BLOCKS, D if gate == "z" else TOKENS],
@@ -164,17 +166,27 @@ def tile_lstmlayer_pa_t_kernel(
                     bufs=3 if gate == "z" else 2,
                 )
             block = slice(P * b, P * (b + 1))
-            if gate == "h":
-                act_codes, act_scales = sr_codes[s], sr_scales[s]
-            else:
-                act_codes, act_scales = s_codes[s], s_scales[s]
             plain = psum_plain.tile([P, TOKENS], F32)
-            mx = psum_mx.tile([P, TOKENS], F32)
-            plain_sb = work.tile([P, TOKENS], F32, bufs=4)
+            plain_sb[gate, s, b] = work.tile([P, TOKENS], F32, name="plain_sb", bufs=4)
             if gate == "z":
                 nc.tensor.matmul(
                     out=plain[:], lhsT=x_t[s][:, block], rhs=u_ready[gate][:], start=True, stop=True
                 )
+                nc.vector.tensor_add(out=plain_sb[gate, s, b][:], in0=plain[:], in1=bz_rows[:])
+            else:
+                nc.tensor.matmul(
+                    out=plain[:], lhsT=u_ready[gate][:, block], rhs=x_t[s][:], start=True, stop=True
+                )
+                nc.scalar.copy(out=plain_sb[gate, s, b][:], in_=plain[:])
+
+        def mx_part(gate, s, b):
+            block = slice(P * b, P * (b + 1))
+            if gate == "h":
+                act_codes, act_scales = sr_codes[s], sr_scales[s]
+            else:
+                act_codes, act_scales = s_codes[s], s_scales[s]
+            mx = psum_mx.tile([P, TOKENS], F32)
+            if gate == "z":
                 nc.tensor.matmul_mx(
                     out=mx[:],
                     lhsT=act_codes[:, block].bitcast(FP8X4),
@@ -184,11 +196,7 @@ def tile_lstmlayer_pa_t_kernel(
                     start=True,
                     stop=True,
                 )
-                nc.vector.tensor_add(out=plain_sb[:], in0=plain[:], in1=bz_rows[:])
             else:
-                nc.tensor.matmul(
-                    out=plain[:], lhsT=u_ready[gate][:, block], rhs=x_t[s][:], start=True, stop=True
-                )
                 nc.tensor.matmul_mx(
                     out=mx[:],
                     lhsT=w_codes[gate][:, block].bitcast(FP8X4),
@@ -198,8 +206,9 @@ def tile_lstmlayer_pa_t_kernel(
                     start=True,
                     stop=True,
                 )
-                nc.scalar.copy(out=plain_sb[:], in_=plain[:])
-            nc.vector.tensor_add(out=gate_tile[gate, s][:, b, :], in0=mx[:], in1=plain_sb[:])
+            nc.vector.tensor_add(
+                out=gate_tile[gate, s][:, b, :], in0=mx[:], in1=plain_sb[gate, s, b][:]
+            )
 
         def tanh(gate, s, b):
             values = gate_tile[gate, s][:, b, :]
@@ -227,10 +236,13 @@ def tile_lstmlayer_pa_t_kernel(
         started = []
 
         def step(gate, s, b):
-            sums(gate, s, b)
+            plain_part(gate, s, b)
             started.append((gate, s, b))
-            if len(started) > TANH_LAG:
-                tanh(*started[len(started) - 1 - TANH_LAG])
+            newest = len(started) - 1
+            if newest >= MX_LAG:
+                mx_part(*started[newest - MX_LAG])
+            if newest >= MX_LAG + TANH_LAG:
+                tanh(*started[newest - MX_LAG - TANH_LAG])
 
         def blend(s, t):
             nc.vector.scalar_tensor_tensor(
@@ -250,11 +262,10 @@ def tile_lstmlayer_pa_t_kernel(
                     in_=gate_tile["g", s][:, t, P * j : P * (j + 1)],
                     identity=ident_f32[:],
                 )
-            columns = gate_tile["z", s][:, :, P * t : P * (t + 1)]
+            block = slice(P * t, P * (t + 1))
+            columns = gate_tile["z", s][:, :, block]
             nc.vector.tensor_sub(out=columns, in0=columns, in1=back[:])
-
-        def store(s):
-            nc.sync.dma_start(out=out_rounds[s], in_=gate_tile["z", s][:])
+            nc.sync.dma_start(out=out_rounds[s][:, :, block], in_=columns)
 
         load_gate("r")
         load_round(0)
@@ -274,6 +285,9 @@ def tile_lstmlayer_pa_t_kernel(
         make_identity(nc, ident_bf16[:])
 
         prepare_gate("r")
+
+        transpose_in(0)
+        quantise_s(0)
 
         bias_sorted = const.tile([P, D], BF16)
         nc.vector.tensor_copy(
@@ -295,8 +309,6 @@ def tile_lstmlayer_pa_t_kernel(
         b_plain = bias_columns(bias_rows, "b_plain")
         b_col = {"r": b_sorted, "g": b_plain, "h": b_plain}
 
-        transpose_in(0)
-        quantise_s(0)
         for t in range(BLOCKS):
             step("r", 0, t)
             if t < 3:
@@ -322,12 +334,12 @@ def tile_lstmlayer_pa_t_kernel(
                 step("h", s, t)
                 if s > 0:
                     finish(s - 1, t)
-            if s > 0:
-                store(s - 1)
 
-        for late in started[len(started) - TANH_LAG :]:
+        for late in started[len(started) - MX_LAG :]:
+            mx_part(*late)
+        for late in started[len(started) - MX_LAG - TANH_LAG :]:
             tanh(*late)
         for t in range(BLOCKS):
             blend(ROUNDS - 1, t)
+        for t in range(BLOCKS):
             finish(ROUNDS - 1, t)
-        store(ROUNDS - 1)

@@ -210,16 +210,26 @@ def tile_lstmlayer_pa_t_kernel(
                 out=gate_tile[gate, s][:, b, :], in0=mx[:], in1=plain_sb[gate, s, b][:]
             )
 
-        def tanh(gate, s, b):
+        def activate(gate, s, b):
             values = gate_tile[gate, s][:, b, :]
             if gate == "z":
                 nc.scalar.activation(out=values, in_=values, func=ACT.Tanh)
                 nc.gpsimd.tensor_tensor(out=values, in0=values, in1=s_nat[s][:, b, :], op=ALU.mult)
-            else:
-                index = BY_FEATURE.index(gate)
+            elif gate == "g":
                 nc.scalar.activation(
-                    out=values, in_=values, func=ACT.Tanh, bias=b_col[gate][:, b, index : index + 1]
+                    out=values,
+                    in_=values,
+                    func=ACT.Sigmoid,
+                    scale=-2.0,
+                    bias=bias_col[gate][:, b : b + 1],
                 )
+            else:
+                nc.scalar.activation(
+                    out=values, in_=values, func=ACT.Tanh, bias=bias_col[gate][:, b : b + 1]
+                )
+            if gate == "h":
+                c_values = gate_tile["g", s][:, b, :]
+                nc.gpsimd.tensor_tensor(out=c_values, in0=c_values, in1=values, op=ALU.mult)
             if gate == "r" and b == BLOCKS - 1:
                 sr_grouped[s] = work.tile(
                     [P, TOKENS, PACK], BF16, name="sr_grouped", align_bytes=64
@@ -242,17 +252,7 @@ def tile_lstmlayer_pa_t_kernel(
             if newest >= MX_LAG:
                 mx_part(*started[newest - MX_LAG])
             if newest >= MX_LAG + TANH_LAG:
-                tanh(*started[newest - MX_LAG - TANH_LAG])
-
-        def blend(s, t):
-            nc.vector.scalar_tensor_tensor(
-                out=gate_tile["g", s][:, t, :],
-                in0=gate_tile["g", s][:, t, :],
-                scalar=1.0,
-                in1=gate_tile["h", s][:, t, :],
-                op0=ALU.subtract,
-                op1=ALU.mult,
-            )
+                activate(*started[newest - MX_LAG - TANH_LAG])
 
         def finish(s, t):
             back = psum_t.tile([P, BLOCKS, P], F32, tag="t")
@@ -264,7 +264,9 @@ def tile_lstmlayer_pa_t_kernel(
                 )
             block = slice(P * t, P * (t + 1))
             columns = gate_tile["z", s][:, :, block]
-            nc.vector.tensor_sub(out=columns, in0=columns, in1=back[:])
+            nc.vector.scalar_tensor_tensor(
+                out=columns, in0=back[:], scalar=2.0, in1=columns, op0=ALU.mult, op1=ALU.add
+            )
             nc.sync.dma_start(out=out_rounds[s][:, :, block], in_=columns)
 
         load_gate("r")
@@ -294,20 +296,20 @@ def tile_lstmlayer_pa_t_kernel(
             out=bias_sorted[:].rearrange("k (u e c) -> k u e c", u=2, e=2),
             in_=bias_rows[:].rearrange("k (u c e) -> k u e c", u=2, e=2),
         )
-
-        def bias_columns(rows, name):
+        bias_col = {}
+        for index, gate in enumerate(BY_FEATURE):
+            rows = bias_sorted if gate == "r" else bias_rows
             bias_bank = psum_t.tile([P, BLOCKS, P], BF16, tag="t")
             for t in range(BLOCKS):
                 nc.tensor.transpose(
                     out=bias_bank[:, t, :], in_=rows[:, P * t : P * (t + 1)], identity=ident_bf16[:]
                 )
-            kept = const.tile([P, BLOCKS, len(BY_FEATURE)], F32, name=name)
-            nc.vector.tensor_copy(out=kept[:], in_=bias_bank[:, :, 0 : len(BY_FEATURE)])
-            return kept
-
-        b_sorted = bias_columns(bias_sorted, "b_sorted")
-        b_plain = bias_columns(bias_rows, "b_plain")
-        b_col = {"r": b_sorted, "g": b_plain, "h": b_plain}
+            bias_col[gate] = const.tile([P, BLOCKS], F32, name="bias_col_%s" % gate)
+            nc.vector.tensor_scalar_mul(
+                out=bias_col[gate][:],
+                in0=bias_bank[:, :, index],
+                scalar1=-2.0 if gate == "g" else 1.0,
+            )
 
         for t in range(BLOCKS):
             step("r", 0, t)
@@ -325,11 +327,9 @@ def tile_lstmlayer_pa_t_kernel(
                 if b == 0 and s + 1 < ROUNDS:
                     quantise_s(s + 1)
             quantise_sr(s)
-            for t in range(BLOCKS):
-                if s + 1 < ROUNDS:
+            if s + 1 < ROUNDS:
+                for t in range(BLOCKS):
                     step("r", s + 1, t)
-                if s > 0:
-                    blend(s - 1, t)
             for t in range(BLOCKS):
                 step("h", s, t)
                 if s > 0:
@@ -338,8 +338,6 @@ def tile_lstmlayer_pa_t_kernel(
         for late in started[len(started) - MX_LAG :]:
             mx_part(*late)
         for late in started[len(started) - MX_LAG - TANH_LAG :]:
-            tanh(*late)
-        for t in range(BLOCKS):
-            blend(ROUNDS - 1, t)
+            activate(*late)
         for t in range(BLOCKS):
             finish(ROUNDS - 1, t)

@@ -40,7 +40,7 @@ def tile_lstmlayer_pa_t_kernel(
         ctx.enter_context(tc.manual_schedule())
         const = ctx.enter_context(tc.tile_pool(name="const", bufs=1))
         stage = ctx.enter_context(tc.tile_pool(name="stage", bufs=4))
-        loads = ctx.enter_context(tc.tile_pool(name="loads", bufs=3))
+        loads = ctx.enter_context(tc.tile_pool(name="loads", bufs=4))
         work = ctx.enter_context(tc.tile_pool(name="work", bufs=2))
         psum_plain = ctx.enter_context(tc.psum_pool(name="psum_plain", bufs=2))
         psum_mx = ctx.enter_context(tc.psum_pool(name="psum_mx", bufs=2))
@@ -53,6 +53,8 @@ def tile_lstmlayer_pa_t_kernel(
         u_ready = {}
         s_nat = {}
         x_nat = {}
+        s_banks = {}
+        x_bank = {}
         s_grouped = {}
         s_codes = {}
         s_scales = {}
@@ -106,14 +108,7 @@ def tile_lstmlayer_pa_t_kernel(
             )
 
         def transpose_in(s):
-            s_grouped[s] = work.tile([P, TOKENS, PACK], BF16, name="s_grouped", align_bytes=64)
-            s_words = (
-                s_grouped[s][:]
-                .rearrange("x m t -> x (m t)")
-                .bitcast(F32)
-                .rearrange("x (m u) -> x m u", u=2)
-            )
-            s_banks = []
+            s_banks[s] = []
             for pair in range(BLOCKS // 2):
                 s_bank = psum_t.tile([P, 2, 2 * P], F32, tag="t")
                 for u in range(2):
@@ -123,30 +118,40 @@ def tile_lstmlayer_pa_t_kernel(
                             in_=s_nat[s][:, 2 * pair + i, :].bitcast(F32)[:, P * u : P * (u + 1)],
                             identity=ident_f32[:],
                         )
-                s_banks.append(s_bank)
-            x_bank = psum_t.tile([P, TOKENS], BF16, tag="t")
+                s_banks[s].append(s_bank)
+            x_bank[s] = psum_t.tile([P, TOKENS], BF16, name="x_bank", tag="t")
             for j in range(BLOCKS):
                 nc.tensor.transpose(
-                    out=x_bank[:, P * j : P * (j + 1)],
+                    out=x_bank[s][:, P * j : P * (j + 1)],
                     in_=x_nat[s][:, j, :],
                     identity=ident_bf16[:],
                 )
-            for pair in range(BLOCKS // 2):
-                nc.scalar.copy(
-                    out=s_words[:, 2 * P * pair : 2 * P * (pair + 1), :],
-                    in_=s_banks[pair][:].rearrange("x u m -> x m u"),
-                )
-            x_t[s] = work.tile([P, TOKENS], BF16, name="x_t")
-            nc.scalar.copy(out=x_t[s][:], in_=x_bank[:])
 
-        def quantise_s(s):
-            s_codes[s] = work.tile([P, TOKENS], U32, name="s_codes", align_bytes=64)
-            s_scales[s] = work.tile([P, TOKENS], U8, name="s_scales", align_bytes=64)
-            nc.vector.quantize_mx(
-                out=s_codes[s][:].bitcast(FP8X4),
-                scales=s_scales[s][:],
-                in_=s_grouped[s][:].rearrange("x m t -> x (m t)"),
-            )
+        def bring_in(s, part):
+            if part == 0:
+                s_grouped[s] = work.tile([P, TOKENS, PACK], BF16, name="s_grouped", align_bytes=64)
+            if part < 2:
+                s_words = (
+                    s_grouped[s][:]
+                    .rearrange("x m t -> x (m t)")
+                    .bitcast(F32)
+                    .rearrange("x (m u) -> x m u", u=2)
+                )
+                nc.vector.tensor_copy(
+                    out=s_words[:, 2 * P * part : 2 * P * (part + 1), :],
+                    in_=s_banks[s][part][:].rearrange("x u m -> x m u"),
+                )
+            elif part == 2:
+                x_t[s] = work.tile([P, TOKENS], BF16, name="x_t", bufs=3)
+                nc.vector.tensor_copy(out=x_t[s][:], in_=x_bank[s][:])
+            else:
+                s_codes[s] = work.tile([P, TOKENS], U32, name="s_codes", align_bytes=64)
+                s_scales[s] = work.tile([P, TOKENS], U8, name="s_scales", align_bytes=64)
+                nc.vector.quantize_mx(
+                    out=s_codes[s][:].bitcast(FP8X4),
+                    scales=s_scales[s][:],
+                    in_=s_grouped[s][:].rearrange("x m t -> x (m t)"),
+                )
 
         def quantise_sr(s):
             sr_codes[s] = work.tile([P, TOKENS], U32, name="sr_codes", align_bytes=64)
@@ -229,7 +234,8 @@ def tile_lstmlayer_pa_t_kernel(
                 )
             if gate == "h":
                 c_values = gate_tile["g", s][:, b, :]
-                nc.gpsimd.tensor_tensor(out=c_values, in0=c_values, in1=values, op=ALU.mult)
+                engine = nc.vector if s == ROUNDS - 1 else nc.gpsimd
+                engine.tensor_tensor(out=c_values, in0=c_values, in1=values, op=ALU.mult)
             if gate == "r" and b == BLOCKS - 1:
                 sr_grouped[s] = work.tile(
                     [P, TOKENS, PACK], BF16, name="sr_grouped", align_bytes=64
@@ -280,6 +286,7 @@ def tile_lstmlayer_pa_t_kernel(
         for gate in ("z", "g", "h"):
             load_gate(gate)
         load_round(1)
+        load_round(2)
 
         ident_f32 = const.tile([P, P], F32)
         make_identity(nc, ident_f32[:])
@@ -289,7 +296,8 @@ def tile_lstmlayer_pa_t_kernel(
         prepare_gate("r")
 
         transpose_in(0)
-        quantise_s(0)
+        for part in range(BLOCKS):
+            bring_in(0, part)
 
         bias_sorted = const.tile([P, D], BF16)
         nc.vector.tensor_copy(
@@ -311,25 +319,27 @@ def tile_lstmlayer_pa_t_kernel(
                 scalar1=-2.0 if gate == "g" else 1.0,
             )
 
+        transpose_in(1)
         for t in range(BLOCKS):
             step("r", 0, t)
+            bring_in(1, t)
             if t < 3:
                 prepare_gate(("z", "g", "h")[t])
 
         for s in range(ROUNDS):
-            if s + 2 < ROUNDS:
-                load_round(s + 2)
-            if s + 1 < ROUNDS:
-                transpose_in(s + 1)
+            if s + 3 < ROUNDS:
+                load_round(s + 3)
             for b in range(BLOCKS):
                 step("z", s, b)
                 step("g", s, b)
-                if b == 0 and s + 1 < ROUNDS:
-                    quantise_s(s + 1)
             quantise_sr(s)
-            if s + 1 < ROUNDS:
-                for t in range(BLOCKS):
+            if s + 2 < ROUNDS:
+                transpose_in(s + 2)
+            for t in range(BLOCKS):
+                if s + 1 < ROUNDS:
                     step("r", s + 1, t)
+                if s + 2 < ROUNDS:
+                    bring_in(s + 2, t)
             for t in range(BLOCKS):
                 step("h", s, t)
                 if s > 0:

@@ -17,11 +17,9 @@ PACK = 4
 TOKENS = 512
 BLOCKS = 4
 ROUNDS = M // TOKENS
-BY_FEATURE = ("r", "g", "h")
-MX_LAG = 1
-TANH_LAG = 2
+GATES = ("r", "z", "g", "h")
 
-FLOPS = 2 * M * D * 4 * (D + DIN)
+FLOPS = 2 * M * D * len(GATES) * (D + DIN)
 
 
 def tile_lstmlayer_pa_t_kernel(
@@ -30,7 +28,7 @@ def tile_lstmlayer_pa_t_kernel(
     nc = tc.nc
     w_dram = {"r": Wr, "z": Wz, "g": Wg, "h": Wh}
     u_dram = {"r": Ur, "z": Uz, "g": Ug, "h": Uh}
-    b_dram = {"r": br, "g": bg, "h": bh}
+    b_dram = {"r": br, "z": bz, "g": bg, "h": bh}
 
     s_rounds = S.rearrange("(s p j) d -> s p j d", p=P, j=BLOCKS)
     x_rounds = X.rearrange("(s p j) d -> s p j d", p=P, j=BLOCKS)
@@ -40,11 +38,11 @@ def tile_lstmlayer_pa_t_kernel(
         ctx.enter_context(tc.manual_schedule())
         const = ctx.enter_context(tc.tile_pool(name="const", bufs=1))
         stage = ctx.enter_context(tc.tile_pool(name="stage", bufs=4))
-        loads = ctx.enter_context(tc.tile_pool(name="loads", bufs=4))
+        loads = ctx.enter_context(tc.tile_pool(name="loads", bufs=3))
         work = ctx.enter_context(tc.tile_pool(name="work", bufs=2))
-        psum_plain = ctx.enter_context(tc.psum_pool(name="psum_plain", bufs=2))
-        psum_mx = ctx.enter_context(tc.psum_pool(name="psum_mx", bufs=2))
-        psum_t = ctx.enter_context(tc.psum_pool(name="psum_t", bufs=4))
+        psum_mx = ctx.enter_context(tc.psum_pool(name="psum_mx", bufs=3))
+        psum_sum = ctx.enter_context(tc.psum_pool(name="psum_sum", bufs=3))
+        psum_t = ctx.enter_context(tc.psum_pool(name="psum_t", bufs=2))
 
         w_raw = {}
         u_raw = {}
@@ -53,8 +51,6 @@ def tile_lstmlayer_pa_t_kernel(
         u_ready = {}
         s_nat = {}
         x_nat = {}
-        s_banks = {}
-        x_bank = {}
         s_grouped = {}
         s_codes = {}
         s_scales = {}
@@ -62,8 +58,8 @@ def tile_lstmlayer_pa_t_kernel(
         sr_grouped = {}
         sr_codes = {}
         sr_scales = {}
+        mx_sb = {}
         gate_tile = {}
-        plain_sb = {}
 
         def load_gate(gate):
             w_raw[gate] = stage.tile([P, PACK, D], BF16, name="w_raw")
@@ -107,8 +103,14 @@ def tile_lstmlayer_pa_t_kernel(
                 in_=w_grouped[:].rearrange("x c t -> x (c t)"),
             )
 
-        def transpose_in(s):
-            s_banks[s] = []
+        def bring_in_s(s):
+            s_grouped[s] = work.tile([P, TOKENS, PACK], BF16, name="s_grouped", align_bytes=64)
+            s_words = (
+                s_grouped[s][:]
+                .rearrange("x m t -> x (m t)")
+                .bitcast(F32)
+                .rearrange("x (m u) -> x m u", u=2)
+            )
             for pair in range(BLOCKS // 2):
                 s_bank = psum_t.tile([P, 2, 2 * P], F32, tag="t")
                 for u in range(2):
@@ -118,80 +120,49 @@ def tile_lstmlayer_pa_t_kernel(
                             in_=s_nat[s][:, 2 * pair + i, :].bitcast(F32)[:, P * u : P * (u + 1)],
                             identity=ident_f32[:],
                         )
-                s_banks[s].append(s_bank)
-            x_bank[s] = psum_t.tile([P, TOKENS], BF16, name="x_bank", tag="t")
+                copy_out(
+                    pair,
+                    s_words[:, 2 * P * pair : 2 * P * (pair + 1), :],
+                    s_bank[:].rearrange("x u m -> x m u"),
+                    None,
+                )
+
+        def bring_in_x(s):
+            x_bank = psum_t.tile([P, TOKENS], BF16, tag="t")
             for j in range(BLOCKS):
                 nc.tensor.transpose(
-                    out=x_bank[s][:, P * j : P * (j + 1)],
-                    in_=x_nat[s][:, j, :],
-                    identity=ident_bf16[:],
+                    out=x_bank[:, P * j : P * (j + 1)], in_=x_nat[s][:, j, :], identity=ident_bf16[:]
                 )
-
-        def bring_in(s, part):
-            if part == 0:
-                s_grouped[s] = work.tile([P, TOKENS, PACK], BF16, name="s_grouped", align_bytes=64)
-            if part < 2:
-                s_words = (
-                    s_grouped[s][:]
-                    .rearrange("x m t -> x (m t)")
-                    .bitcast(F32)
-                    .rearrange("x (m u) -> x m u", u=2)
-                )
-                nc.vector.tensor_copy(
-                    out=s_words[:, 2 * P * part : 2 * P * (part + 1), :],
-                    in_=s_banks[s][part][:].rearrange("x u m -> x m u"),
-                )
-            elif part == 2:
-                x_t[s] = work.tile([P, TOKENS], BF16, name="x_t", bufs=3)
-                nc.vector.tensor_copy(out=x_t[s][:], in_=x_bank[s][:])
-            else:
-                s_codes[s] = work.tile([P, TOKENS], U32, name="s_codes", align_bytes=64)
-                s_scales[s] = work.tile([P, TOKENS], U8, name="s_scales", align_bytes=64)
-                nc.vector.quantize_mx(
-                    out=s_codes[s][:].bitcast(FP8X4),
-                    scales=s_scales[s][:],
-                    in_=s_grouped[s][:].rearrange("x m t -> x (m t)"),
-                )
-
-        def quantise_sr(s):
-            sr_codes[s] = work.tile([P, TOKENS], U32, name="sr_codes", align_bytes=64)
-            sr_scales[s] = work.tile([P, TOKENS], U8, name="sr_scales", align_bytes=64)
+            x_t[s] = work.tile([P, TOKENS], BF16, name="x_t", bufs=3)
+            copy_out(0, x_t[s][:], x_bank[:], None)
+            s_codes[s] = work.tile([P, TOKENS], U32, name="s_codes", align_bytes=64)
+            s_scales[s] = work.tile([P, TOKENS], U8, name="s_scales", align_bytes=64)
             nc.vector.quantize_mx(
-                out=sr_codes[s][:].bitcast(FP8X4),
-                scales=sr_scales[s][:],
-                in_=sr_grouped[s][:].rearrange("x m t -> x (m t)"),
+                out=s_codes[s][:].bitcast(FP8X4),
+                scales=s_scales[s][:],
+                in_=s_grouped[s][:].rearrange("x m t -> x (m t)"),
             )
 
-        def plain_part(gate, s, b):
-            if b == 0:
-                gate_tile[gate, s] = work.tile(
-                    [P, BLOCKS, D if gate == "z" else TOKENS],
-                    F32,
-                    name=gate,
-                    bufs=3 if gate == "z" else 2,
-                )
-            block = slice(P * b, P * (b + 1))
-            plain = psum_plain.tile([P, TOKENS], F32)
-            plain_sb[gate, s, b] = work.tile([P, TOKENS], F32, name="plain_sb", bufs=4)
-            if gate == "z":
-                nc.tensor.matmul(
-                    out=plain[:], lhsT=x_t[s][:, block], rhs=u_ready[gate][:], start=True, stop=True
-                )
-                nc.vector.tensor_add(out=plain_sb[gate, s, b][:], in0=plain[:], in1=bz_rows[:])
+        def copy_out(number, dst, bank, bias):
+            if number % 2 == 0 and bias is None:
+                nc.scalar.copy(out=dst, in_=bank)
+            elif number % 2 == 0:
+                nc.scalar.activation(out=dst, in_=bank, func=ACT.Identity, bias=bias)
+            elif bias is None:
+                nc.vector.tensor_copy(out=dst, in_=bank)
             else:
-                nc.tensor.matmul(
-                    out=plain[:], lhsT=u_ready[gate][:, block], rhs=x_t[s][:], start=True, stop=True
-                )
-                nc.scalar.copy(out=plain_sb[gate, s, b][:], in_=plain[:])
+                nc.vector.tensor_scalar_add(out=dst, in0=bank, scalar1=bias)
 
-        def mx_part(gate, s, b):
-            block = slice(P * b, P * (b + 1))
+        def mx_product(gate, s, a):
+            if a == 0:
+                mx_sb[gate, s] = work.tile([P, BLOCKS, TOKENS], F32, name="mx_sb")
+            block = slice(P * a, P * (a + 1))
             if gate == "h":
                 act_codes, act_scales = sr_codes[s], sr_scales[s]
             else:
                 act_codes, act_scales = s_codes[s], s_scales[s]
             mx = psum_mx.tile([P, TOKENS], F32)
-            if gate == "z":
+            if gate == "r":
                 nc.tensor.matmul_mx(
                     out=mx[:],
                     lhsT=act_codes[:, block].bitcast(FP8X4),
@@ -201,6 +172,7 @@ def tile_lstmlayer_pa_t_kernel(
                     start=True,
                     stop=True,
                 )
+                copy_out(a, mx_sb[gate, s][:, a, :], mx[:], None)
             else:
                 nc.tensor.matmul_mx(
                     out=mx[:],
@@ -211,82 +183,93 @@ def tile_lstmlayer_pa_t_kernel(
                     start=True,
                     stop=True,
                 )
-            nc.vector.tensor_add(
-                out=gate_tile[gate, s][:, b, :], in0=mx[:], in1=plain_sb[gate, s, b][:]
-            )
+                copy_out(a, mx_sb[gate, s][:, a, :], mx[:], bias_col[gate][:, a : a + 1])
 
-        def activate(gate, s, b):
-            values = gate_tile[gate, s][:, b, :]
-            if gate == "z":
-                nc.scalar.activation(out=values, in_=values, func=ACT.Tanh)
-                nc.gpsimd.tensor_tensor(out=values, in0=values, in1=s_nat[s][:, b, :], op=ALU.mult)
-            elif gate == "g":
+        def gate_block(gate, s, b):
+            if b == 0:
+                gate_tile[gate, s] = work.tile(
+                    [P, BLOCKS, TOKENS], F32, name=gate, bufs=3 if gate == "z" else 2
+                )
+            block = slice(P * b, P * (b + 1))
+            total = psum_sum.tile([P, TOKENS], F32)
+            if gate == "r":
+                nc.tensor.matmul(
+                    out=total[:], lhsT=u_ready[gate][:, block], rhs=x_t[s][:], start=True, stop=False
+                )
+            else:
+                nc.tensor.matmul(
+                    out=total[:], lhsT=x_t[s][:, block], rhs=u_ready[gate][:], start=True, stop=False
+                )
+            for a in range(BLOCKS):
+                nc.tensor.matmul(
+                    out=total[:, P * a : P * (a + 1)],
+                    lhsT=mx_sb[gate, s][:, a, block],
+                    rhs=ident_f32[:],
+                    is_transpose=True,
+                    start=False,
+                    stop=(a == BLOCKS - 1),
+                )
+            if gate == "r":
                 nc.scalar.activation(
-                    out=values,
-                    in_=values,
-                    func=ACT.Sigmoid,
-                    scale=-2.0,
+                    out=gate_tile[gate, s][:, b, :],
+                    in_=total[:],
+                    func=ACT.Tanh,
                     bias=bias_col[gate][:, b : b + 1],
                 )
             else:
-                nc.scalar.activation(
-                    out=values, in_=values, func=ACT.Tanh, bias=bias_col[gate][:, b : b + 1]
-                )
-            if gate == "h":
-                c_values = gate_tile["g", s][:, b, :]
-                engine = nc.vector if s == ROUNDS - 1 else nc.gpsimd
-                engine.tensor_tensor(out=c_values, in0=c_values, in1=values, op=ALU.mult)
-            if gate == "r" and b == BLOCKS - 1:
+                nc.scalar.activation(out=gate_tile[gate, s][:, b, :], in_=total[:], func=ACT.Tanh)
+
+        def follow_up(gate, s):
+            if gate == "r":
                 sr_grouped[s] = work.tile(
                     [P, TOKENS, PACK], BF16, name="sr_grouped", align_bytes=64
                 )
-                for i in range(2):
-                    part = slice(TOKENS // 2 * i, TOKENS // 2 * (i + 1))
-                    nc.gpsimd.tensor_tensor(
-                        out=sr_grouped[s][:, part, :],
-                        in0=s_grouped[s][:, part, :],
-                        in1=gate_tile[gate, s][:, :, part].rearrange("x t m -> x m t"),
-                        op=ALU.mult,
-                    )
-
-        started = []
-
-        def step(gate, s, b):
-            plain_part(gate, s, b)
-            started.append((gate, s, b))
-            newest = len(started) - 1
-            if newest >= MX_LAG:
-                mx_part(*started[newest - MX_LAG])
-            if newest >= MX_LAG + TANH_LAG:
-                activate(*started[newest - MX_LAG - TANH_LAG])
-
-        def finish(s, t):
-            back = psum_t.tile([P, BLOCKS, P], F32, tag="t")
-            for j in range(BLOCKS):
-                nc.tensor.transpose(
-                    out=back[:, j, :],
-                    in_=gate_tile["g", s][:, t, P * j : P * (j + 1)],
-                    identity=ident_f32[:],
+                nc.vector.tensor_tensor(
+                    out=sr_grouped[s][:],
+                    in0=s_grouped[s][:],
+                    in1=gate_tile["r", s][:].rearrange("x t m -> x m t"),
+                    op=ALU.mult,
                 )
-            block = slice(P * t, P * (t + 1))
-            columns = gate_tile["z", s][:, :, block]
-            nc.vector.scalar_tensor_tensor(
-                out=columns, in0=back[:], scalar=2.0, in1=columns, op0=ALU.mult, op1=ALU.add
+            if gate == "z":
+                nc.vector.tensor_mul(
+                    out=gate_tile["z", s][:], in0=gate_tile["z", s][:], in1=s_nat[s][:]
+                )
+            if gate == "h":
+                nc.vector.scalar_tensor_tensor(
+                    out=gate_tile["g", s][:],
+                    in0=gate_tile["g", s][:],
+                    scalar=1.0,
+                    in1=gate_tile["h", s][:],
+                    op0=ALU.subtract,
+                    op1=ALU.mult,
+                )
+            if gate == "g" and s > 0:
+                finish(s - 1)
+
+        def quantise_sr(s):
+            sr_codes[s] = work.tile([P, TOKENS], U32, name="sr_codes", align_bytes=64)
+            sr_scales[s] = work.tile([P, TOKENS], U8, name="sr_scales", align_bytes=64)
+            nc.vector.quantize_mx(
+                out=sr_codes[s][:].bitcast(FP8X4),
+                scales=sr_scales[s][:],
+                in_=sr_grouped[s][:].rearrange("x m t -> x (m t)"),
             )
-            nc.sync.dma_start(out=out_rounds[s][:, :, block], in_=columns)
+
+        def finish(s):
+            nc.vector.tensor_sub(
+                out=gate_tile["z", s][:], in0=gate_tile["z", s][:], in1=gate_tile["g", s][:]
+            )
+            nc.sync.dma_start(out=out_rounds[s], in_=gate_tile["z", s][:])
 
         load_gate("r")
         load_round(0)
         bias_rows = const.tile([P, D], BF16)
         nc.vector.memset(bias_rows[:], 0.0)
-        for index, gate in enumerate(BY_FEATURE):
+        for index, gate in enumerate(GATES):
             nc.sync.dma_start(out=bias_rows[index : index + 1, :], in_=b_dram[gate])
-        bz_rows = const.tile([P, D], BF16)
-        nc.sync.dma_start(out=bz_rows[:], in_=bz.rearrange("o d -> (o d)").partition_broadcast(P))
         for gate in ("z", "g", "h"):
             load_gate(gate)
         load_round(1)
-        load_round(2)
 
         ident_f32 = const.tile([P, P], F32)
         make_identity(nc, ident_f32[:])
@@ -294,10 +277,8 @@ def tile_lstmlayer_pa_t_kernel(
         make_identity(nc, ident_bf16[:])
 
         prepare_gate("r")
-
-        transpose_in(0)
-        for part in range(BLOCKS):
-            bring_in(0, part)
+        bring_in_s(0)
+        bring_in_x(0)
 
         bias_sorted = const.tile([P, D], BF16)
         nc.vector.tensor_copy(
@@ -305,49 +286,49 @@ def tile_lstmlayer_pa_t_kernel(
             in_=bias_rows[:].rearrange("k (u c e) -> k u e c", u=2, e=2),
         )
         bias_col = {}
-        for index, gate in enumerate(BY_FEATURE):
-            rows = bias_sorted if gate == "r" else bias_rows
+        for rows, gates in ((bias_sorted, ("r",)), (bias_rows, ("z", "g", "h"))):
             bias_bank = psum_t.tile([P, BLOCKS, P], BF16, tag="t")
             for t in range(BLOCKS):
                 nc.tensor.transpose(
                     out=bias_bank[:, t, :], in_=rows[:, P * t : P * (t + 1)], identity=ident_bf16[:]
                 )
-            bias_col[gate] = const.tile([P, BLOCKS], F32, name="bias_col_%s" % gate)
-            nc.vector.tensor_scalar_mul(
-                out=bias_col[gate][:],
-                in0=bias_bank[:, :, index],
-                scalar1=-2.0 if gate == "g" else 1.0,
-            )
+            for gate in gates:
+                bias_col[gate] = const.tile([P, BLOCKS], F32, name="bias_col_%s" % gate)
+                nc.vector.tensor_copy(
+                    out=bias_col[gate][:], in_=bias_bank[:, :, GATES.index(gate)]
+                )
+        prepare_gate("z")
 
-        transpose_in(1)
-        for t in range(BLOCKS):
-            step("r", 0, t)
-            bring_in(1, t)
-            if t < 3:
-                prepare_gate(("z", "g", "h")[t])
-
+        order = [("r", 0)]
         for s in range(ROUNDS):
-            if s + 3 < ROUNDS:
-                load_round(s + 3)
-            for b in range(BLOCKS):
-                step("z", s, b)
-                step("g", s, b)
-            quantise_sr(s)
-            if s + 2 < ROUNDS:
-                transpose_in(s + 2)
-            for t in range(BLOCKS):
-                if s + 1 < ROUNDS:
-                    step("r", s + 1, t)
-                if s + 2 < ROUNDS:
-                    bring_in(s + 2, t)
-            for t in range(BLOCKS):
-                step("h", s, t)
-                if s > 0:
-                    finish(s - 1, t)
+            order.append(("z", s))
+            order.append(("g", s))
+            if s + 1 < ROUNDS:
+                order.append(("r", s + 1))
+            order.append(("h", s))
 
-        for late in started[len(started) - MX_LAG :]:
-            mx_part(*late)
-        for late in started[len(started) - MX_LAG - TANH_LAG :]:
-            activate(*late)
-        for t in range(BLOCKS):
-            finish(ROUNDS - 1, t)
+        for a in range(BLOCKS):
+            mx_product("r", 0, a)
+        for i, (gate, s) in enumerate(order):
+            if gate == "z" and s + 2 < ROUNDS:
+                load_round(s + 2)
+            if i >= 2:
+                follow_up(*order[i - 2])
+            for first in (0, 2):
+                if i + 1 < len(order):
+                    mx_product(*order[i + 1], first)
+                    mx_product(*order[i + 1], first + 1)
+                gate_block(gate, s, first)
+                gate_block(gate, s, first + 1)
+            if i + 3 < len(order) and order[i + 3][0] == "r":
+                bring_in_s(order[i + 3][1])
+            if i + 2 < len(order) and order[i + 2][0] == "r":
+                bring_in_x(order[i + 2][1])
+            if i >= 2 and order[i - 2][0] == "r":
+                quantise_sr(order[i - 2][1])
+            if i < 2:
+                prepare_gate(("g", "h")[i])
+
+        follow_up(*order[len(order) - 2])
+        follow_up(*order[len(order) - 1])
+        finish(ROUNDS - 1)

from contextlib import ExitStack

import concourse.mybir as mybir
from concourse.masks import make_identity

F32 = mybir.dt.float32
BF16 = mybir.dt.bfloat16
U32 = mybir.dt.uint32
U8 = mybir.dt.uint8
FP8X4 = mybir.dt.float8_e4m3fn_x4
ALU = mybir.AluOpType
ACT = mybir.ActivationFunctionType

M, DIN, D = 4096, 128, 512
P = 128
PACK = 4
TOKENS = 512
BLOCKS = 4
ROUNDS = M // TOKENS
GATES = ("r", "z", "g", "h")

FLOPS = 2 * M * D * len(GATES) * (D + DIN)


def tile_lstmlayer_pa_t_kernel(
    tc, S, X, Uz, Ug, Ur, Uh, Wz, Wg, Wr, Wh, bz, bg, br, bh, out
):
    nc = tc.nc
    w_dram = {"r": Wr, "z": Wz, "g": Wg, "h": Wh}
    u_dram = {"r": Ur, "z": Uz, "g": Ug, "h": Uh}
    b_dram = {"r": br, "z": bz, "g": bg, "h": bh}

    s_rounds = S.rearrange("(s p j) d -> s p j d", p=P, j=BLOCKS)
    x_rounds = X.rearrange("(s p j) d -> s p j d", p=P, j=BLOCKS)
    out_rounds = out.rearrange("(s p j) d -> s p j d", p=P, j=BLOCKS)

    with ExitStack() as ctx:
        ctx.enter_context(tc.manual_schedule())
        const = ctx.enter_context(tc.tile_pool(name="const", bufs=1))
        stage = ctx.enter_context(tc.tile_pool(name="stage", bufs=4))
        loads = ctx.enter_context(tc.tile_pool(name="loads", bufs=3))
        work = ctx.enter_context(tc.tile_pool(name="work", bufs=2))
        psum_mx = ctx.enter_context(tc.psum_pool(name="psum_mx", bufs=3))
        psum_sum = ctx.enter_context(tc.psum_pool(name="psum_sum", bufs=3))
        psum_t = ctx.enter_context(tc.psum_pool(name="psum_t", bufs=2))

        w_raw = {}
        u_raw = {}
        w_codes = {}
        w_scales = {}
        u_ready = {}
        s_nat = {}
        x_nat = {}
        s_grouped = {}
        s_codes = {}
        s_scales = {}
        x_t = {}
        sr_grouped = {}
        sr_codes = {}
        sr_scales = {}
        mx_sb = {}
        gate_tile = {}

        def load_gate(gate):
            w_raw[gate] = stage.tile([P, PACK, D], BF16, name="w_raw")
            nc.sync.dma_start(
                out=w_raw[gate][:].rearrange("x (u e) c -> x u e c", u=2),
                in_=w_dram[gate].rearrange("(u x e) c -> x u e c", u=2, e=2),
            )
            u_raw[gate] = const.tile([P, D], BF16, name="u_raw_%s" % gate)
            nc.sync.dma_start(out=u_raw[gate][:], in_=u_dram[gate])

        def load_round(s):
            s_nat[s] = loads.tile([P, BLOCKS, D], BF16, name="s_nat")
            nc.sync.dma_start(out=s_nat[s][:], in_=s_rounds[s])
            x_nat[s] = loads.tile([P, BLOCKS, DIN], BF16, name="x_nat")
            nc.sync.dma_start(out=x_nat[s][:], in_=x_rounds[s])

        def prepare_gate(gate):
            w_grouped = stage.tile([P, D, PACK], BF16, align_bytes=64, bufs=2)
            if gate == "r":
                for u in range(2):
                    half = slice(2 * P * u, 2 * P * (u + 1))
                    nc.vector.tensor_copy(
                        out=w_grouped[:, half, :].rearrange("x (e c) t -> x e c t", e=2),
                        in_=w_raw[gate][:, :, half].rearrange("x t (c e) -> x e c t", e=2),
                    )
                u_ready[gate] = const.tile([P, D], BF16, name="u_sorted")
                nc.vector.tensor_copy(
                    out=u_ready[gate][:].rearrange("k (u e c) -> k u e c", u=2, e=2),
                    in_=u_raw[gate][:].rearrange("k (u c e) -> k u e c", u=2, e=2),
                )
            else:
                nc.vector.tensor_copy(
                    out=w_grouped[:], in_=w_raw[gate][:].rearrange("x t c -> x c t")
                )
                u_ready[gate] = u_raw[gate]
            w_codes[gate] = const.tile([P, D], U32, name="w_codes_%s" % gate, align_bytes=64)
            w_scales[gate] = const.tile([P, D], U8, name="w_scales_%s" % gate, align_bytes=64)
            nc.vector.quantize_mx(
                out=w_codes[gate][:].bitcast(FP8X4),
                scales=w_scales[gate][:],
                in_=w_grouped[:].rearrange("x c t -> x (c t)"),
            )

        def bring_in_s(s):
            s_grouped[s] = work.tile([P, TOKENS, PACK], BF16, name="s_grouped", align_bytes=64)
            s_words = (
                s_grouped[s][:]
                .rearrange("x m t -> x (m t)")
                .bitcast(F32)
                .rearrange("x (m u) -> x m u", u=2)
            )
            for pair in range(BLOCKS // 2):
                s_bank = psum_t.tile([P, 2, 2 * P], F32, tag="t")
                for u in range(2):
                    for i in range(2):
                        nc.tensor.transpose(
                            out=s_bank[:, u, P * i : P * (i + 1)],
                            in_=s_nat[s][:, 2 * pair + i, :].bitcast(F32)[:, P * u : P * (u + 1)],
                            identity=ident_f32[:],
                        )
                copy_out(
                    pair,
                    s_words[:, 2 * P * pair : 2 * P * (pair + 1), :],
                    s_bank[:].rearrange("x u m -> x m u"),
                    None,
                )

        def bring_in_x(s):
            x_bank = psum_t.tile([P, TOKENS], BF16, tag="t")
            for j in range(BLOCKS):
                nc.tensor.transpose(
                    out=x_bank[:, P * j : P * (j + 1)], in_=x_nat[s][:, j, :], identity=ident_bf16[:]
                )
            x_t[s] = work.tile([P, TOKENS], BF16, name="x_t", bufs=3)
            copy_out(0, x_t[s][:], x_bank[:], None)
            s_codes[s] = work.tile([P, TOKENS], U32, name="s_codes", align_bytes=64)
            s_scales[s] = work.tile([P, TOKENS], U8, name="s_scales", align_bytes=64)
            nc.vector.quantize_mx(
                out=s_codes[s][:].bitcast(FP8X4),
                scales=s_scales[s][:],
                in_=s_grouped[s][:].rearrange("x m t -> x (m t)"),
            )

        def copy_out(number, dst, bank, bias):
            if number % 2 == 0 and bias is None:
                nc.scalar.copy(out=dst, in_=bank)
            elif number % 2 == 0:
                nc.scalar.activation(out=dst, in_=bank, func=ACT.Identity, bias=bias)
            elif bias is None:
                nc.vector.tensor_copy(out=dst, in_=bank)
            else:
                nc.vector.tensor_scalar_add(out=dst, in0=bank, scalar1=bias)

        def mx_product(gate, s, a):
            if a == 0:
                mx_sb[gate, s] = work.tile([P, BLOCKS, TOKENS], F32, name="mx_sb")
            block = slice(P * a, P * (a + 1))
            if gate == "h":
                act_codes, act_scales = sr_codes[s], sr_scales[s]
            else:
                act_codes, act_scales = s_codes[s], s_scales[s]
            mx = psum_mx.tile([P, TOKENS], F32)
            if gate == "r":
                nc.tensor.matmul_mx(
                    out=mx[:],
                    lhsT=act_codes[:, block].bitcast(FP8X4),
                    lhsT_scale=act_scales[:, block],
                    rhs=w_codes[gate][:].bitcast(FP8X4),
                    rhs_scale=w_scales[gate][:],
                    start=True,
                    stop=True,
                )
                copy_out(a, mx_sb[gate, s][:, a, :], mx[:], None)
            else:
                nc.tensor.matmul_mx(
                    out=mx[:],
                    lhsT=w_codes[gate][:, block].bitcast(FP8X4),
                    lhsT_scale=w_scales[gate][:, block],
                    rhs=act_codes[:].bitcast(FP8X4),
                    rhs_scale=act_scales[:],
                    start=True,
                    stop=True,
                )
                copy_out(a, mx_sb[gate, s][:, a, :], mx[:], bias_col[gate][:, a : a + 1])

        def gate_block(gate, s, b):
            if b == 0:
                gate_tile[gate, s] = work.tile(
                    [P, BLOCKS, TOKENS], F32, name=gate, bufs=3 if gate == "z" else 2
                )
            block = slice(P * b, P * (b + 1))
            total = psum_sum.tile([P, TOKENS], F32)
            if gate == "r":
                nc.tensor.matmul(
                    out=total[:], lhsT=u_ready[gate][:, block], rhs=x_t[s][:], start=True, stop=False
                )
            else:
                nc.tensor.matmul(
                    out=total[:], lhsT=x_t[s][:, block], rhs=u_ready[gate][:], start=True, stop=False
                )
            for a in range(BLOCKS):
                nc.tensor.matmul(
                    out=total[:, P * a : P * (a + 1)],
                    lhsT=mx_sb[gate, s][:, a, block],
                    rhs=ident_f32[:],
                    is_transpose=True,
                    start=False,
                    stop=(a == BLOCKS - 1),
                )
            if gate == "r":
                nc.scalar.activation(
                    out=gate_tile[gate, s][:, b, :],
                    in_=total[:],
                    func=ACT.Tanh,
                    bias=bias_col[gate][:, b : b + 1],
                )
            else:
                nc.scalar.activation(out=gate_tile[gate, s][:, b, :], in_=total[:], func=ACT.Tanh)

        def follow_up(gate, s):
            if gate == "r":
                sr_grouped[s] = work.tile(
                    [P, TOKENS, PACK], BF16, name="sr_grouped", align_bytes=64
                )
                nc.vector.tensor_tensor(
                    out=sr_grouped[s][:],
                    in0=s_grouped[s][:],
                    in1=gate_tile["r", s][:].rearrange("x t m -> x m t"),
                    op=ALU.mult,
                )
            if gate == "z":
                nc.vector.tensor_mul(
                    out=gate_tile["z", s][:], in0=gate_tile["z", s][:], in1=s_nat[s][:]
                )
            if gate == "h":
                nc.vector.scalar_tensor_tensor(
                    out=gate_tile["g", s][:],
                    in0=gate_tile["g", s][:],
                    scalar=1.0,
                    in1=gate_tile["h", s][:],
                    op0=ALU.subtract,
                    op1=ALU.mult,
                )
            if gate == "g" and s > 0:
                finish(s - 1)

        def quantise_sr(s):
            sr_codes[s] = work.tile([P, TOKENS], U32, name="sr_codes", align_bytes=64)
            sr_scales[s] = work.tile([P, TOKENS], U8, name="sr_scales", align_bytes=64)
            nc.vector.quantize_mx(
                out=sr_codes[s][:].bitcast(FP8X4),
                scales=sr_scales[s][:],
                in_=sr_grouped[s][:].rearrange("x m t -> x (m t)"),
            )

        def finish(s):
            nc.vector.tensor_sub(
                out=gate_tile["z", s][:], in0=gate_tile["z", s][:], in1=gate_tile["g", s][:]
            )
            nc.sync.dma_start(out=out_rounds[s], in_=gate_tile["z", s][:])

        load_gate("r")
        load_round(0)
        bias_rows = const.tile([P, D], BF16)
        nc.vector.memset(bias_rows[:], 0.0)
        for index, gate in enumerate(GATES):
            nc.sync.dma_start(out=bias_rows[index : index + 1, :], in_=b_dram[gate])
        for gate in ("z", "g", "h"):
            load_gate(gate)
        load_round(1)

        ident_f32 = const.tile([P, P], F32)
        make_identity(nc, ident_f32[:])
        ident_bf16 = const.tile([P, P], BF16)
        make_identity(nc, ident_bf16[:])

        prepare_gate("r")
        bring_in_s(0)
        bring_in_x(0)

        bias_sorted = const.tile([P, D], BF16)
        nc.vector.tensor_copy(
            out=bias_sorted[:].rearrange("k (u e c) -> k u e c", u=2, e=2),
            in_=bias_rows[:].rearrange("k (u c e) -> k u e c", u=2, e=2),
        )
        bias_col = {}
        for rows, gates in ((bias_sorted, ("r",)), (bias_rows, ("z", "g", "h"))):
            bias_bank = psum_t.tile([P, BLOCKS, P], BF16, tag="t")
            for t in range(BLOCKS):
                nc.tensor.transpose(
                    out=bias_bank[:, t, :], in_=rows[:, P * t : P * (t + 1)], identity=ident_bf16[:]
                )
            for gate in gates:
                bias_col[gate] = const.tile([P, BLOCKS], F32, name="bias_col_%s" % gate)
                nc.vector.tensor_copy(
                    out=bias_col[gate][:], in_=bias_bank[:, :, GATES.index(gate)]
                )
        prepare_gate("z")

        order = [("r", 0)]
        for s in range(ROUNDS):
            order.append(("z", s))
            order.append(("g", s))
            if s + 1 < ROUNDS:
                order.append(("r", s + 1))
            order.append(("h", s))

        for a in range(BLOCKS):
            mx_product("r", 0, a)
        for i, (gate, s) in enumerate(order):
            if gate == "z" and s + 2 < ROUNDS:
                load_round(s + 2)
            if i >= 2:
                follow_up(*order[i - 2])
            for first in (0, 2):
                if i + 1 < len(order):
                    mx_product(*order[i + 1], first)
                    mx_product(*order[i + 1], first + 1)
                gate_block(gate, s, first)
                gate_block(gate, s, first + 1)
            if i + 3 < len(order) and order[i + 3][0] == "r":
                bring_in_s(order[i + 3][1])
            if i + 2 < len(order) and order[i + 2][0] == "r":
                bring_in_x(order[i + 2][1])
            if i >= 2 and order[i - 2][0] == "r":
                quantise_sr(order[i - 2][1])
            if i < 2:
                prepare_gate(("g", "h")[i])

        follow_up(*order[len(order) - 2])
        follow_up(*order[len(order) - 1])
        finish(ROUNDS - 1)
